import numpy as np
import ml_dtypes


def mxq(x, axis, fmt="e4m3"):
    dtype, down = {"e4m3": (ml_dtypes.float8_e4m3fn, 7), "e5m2": (ml_dtypes.float8_e5m2, 14)}[fmt]
    v = np.moveaxis(np.asarray(x, np.float32).astype(ml_dtypes.bfloat16).astype(np.float64), axis, -1)
    blocks = v.reshape(v.shape[:-1] + (-1, 32))
    amax = np.abs(blocks).max(-1, keepdims=True)
    byte = np.maximum(np.where(amax > 0, np.frexp(amax)[1] - 1 + 127, 0) - down, 1)
    scale = np.exp2(byte - 127.0)
    codes = (blocks / scale).astype(np.float32).astype(dtype).astype(np.float64)
    return np.moveaxis((codes * scale).reshape(v.shape), -1, axis)


WIDE = False


def mx_kscale(k):
    if not WIDE:
        return np.ones(k)
    levels = np.array([10, -10, 5, -5, 0])
    if k % 512:
        return np.exp2(np.random.permutation(np.resize(levels, k // 32))).repeat(32)
    a = np.empty((k // 512, 16))
    for p in range(k // 512):
        a[p, :8] = np.random.permutation(np.resize(levels, 8))
        for g in range(8):
            far = levels[np.abs(levels - a[p, g]) >= 10]
            a[p, g + 8] = far[np.random.randint(len(far))]
    return np.exp2(a.ravel()).repeat(32)


BF16 = ml_dtypes.bfloat16


def bf(x):
    return np.asarray(x, np.float32).astype(BF16)


def f64(x):
    return np.asarray(x).astype(np.float64)


B, L, S, D, H = 2, 768, 768, 1024, 2
ITER = 3
E = D // H
QS = 1.4 / E ** 0.25


def setup_inputs():
    s = np.tile(mx_kscale(E), H)
    t = mx_kscale(D)
    q = (np.random.standard_normal((B, L, D)) + 0.35 * np.random.standard_normal(D)) * QS
    k = (np.random.standard_normal((B, S, D)) + 0.35 * np.random.standard_normal(D)) * QS
    return {"q_proj": bf(q * s), "k_proj": bf(k / s),
            "values": bf(np.random.standard_normal((B, S, D)) * t),
            "Wv": bf(np.random.standard_normal((D, D)) / np.sqrt(D) / t[:, None]),
            "bv": bf(np.random.standard_normal(D) * 0.2)}


def reference(q_proj, k_proj, values, Wv, bv):
    qh = mxq(f64(q_proj).reshape(B, L, H, E).transpose(0, 2, 1, 3), 3, "e4m3")
    kh = mxq(f64(k_proj).reshape(B, S, H, E).transpose(0, 2, 3, 1), 2, "e4m3")
    v = ((mxq(f64(values), 2, "e4m3") @ mxq(f64(Wv), 0, "e4m3")) + f64(bv)).reshape(B, S, H, E)
    attn_list = []
    acc = np.zeros((B, S, H, E))
    for i in range(ITER):
        stride = i + 1
        attn = qh[:, :, ::stride] @ kh
        attn_list.append(attn)
        e = np.exp(attn - attn.max(-1, keepdims=True))
        att = e / e.sum(-1, keepdims=True)
        colsum = att.sum(2)
        acc = acc + v * colsum.transpose(0, 2, 1)[..., None]
    return ((acc / ITER).reshape(B, S, D), *attn_list)

@@ -1,0 +1,372 @@
+from contextlib import ExitStack
+
+import concourse.mybir as mybir
+from concourse.masks import make_identity
+
+F32 = mybir.dt.float32
+BF16 = mybir.dt.bfloat16
+U32 = mybir.dt.uint32
+U8 = mybir.dt.uint8
+FP8X4 = mybir.dt.float8_e4m3fn_x4
+ALU = mybir.AluOpType
+ACT = mybir.ActivationFunctionType
+
+B, L, S, D, H = 2, 768, 768, 1024, 2
+E = D // H
+STRIDES = (1, 2, 3)
+
+P = 128
+PACK = 4
+K_PASS = P * PACK
+PASSES = D // K_PASS
+TILES = L // P
+PAIRS = TILES // 2
+BANK = 512
+REST = S - BANK
+REPEAT = 8
+
+assert E == K_PASS and E == BANK and L == S
+assert all(TILES % stride == 0 for stride in STRIDES)
+
+FLOPS = 2 * B * H * L * S * E + 2 * B * S * D * D
+
+
+def tile_trendattentionlayer_pa_kernel(
+    tc, q_proj, k_proj, values, Wv, bv, out_0, out_1, out_2, out_3
+):
+    nc = tc.nc
+    attn_out = {1: out_1, 2: out_2, 3: out_3}
+
+    with ExitStack() as ctx:
+        consts = ctx.enter_context(tc.tile_pool(name="consts", bufs=1))
+        raw = ctx.enter_context(tc.tile_pool(name="raw", bufs=B))
+        stage = ctx.enter_context(tc.tile_pool(name="stage", bufs=2))
+        mx = ctx.enter_context(tc.tile_pool(name="mx", bufs=2))
+        logit_pool = ctx.enter_context(tc.tile_pool(name="logit_pool", bufs=6))
+        expo_pool = ctx.enter_context(tc.tile_pool(name="expo_pool", bufs=4))
+        low_pool = ctx.enter_context(tc.tile_pool(name="low_pool", bufs=4))
+        gated_pool = ctx.enter_context(tc.tile_pool(name="gated_pool", bufs=10))
+        small = ctx.enter_context(tc.tile_pool(name="small", bufs=4))
+        psum_two = ctx.enter_context(tc.psum_pool(name="psum_two", bufs=2))
+        psum_one = ctx.enter_context(tc.psum_pool(name="psum_one", bufs=1))
+        ctx.enter_context(tc.manual_schedule())
+
+        def load_rows(source, pattern, tag):
+            rows = raw.tile([P, TILES, D], BF16, tag=tag)
+            view = source.rearrange(pattern, p=P)
+            for pair in range(PAIRS):
+                piece = slice(2 * pair, 2 * pair + 2)
+                nc.sync.dma_start(out=rows[:, piece, :], in_=view[:, piece, :])
+            return rows
+
+        k_raw = [load_rows(k_proj[0], "(c p) d -> p c d", "k_raw")]
+        bias_rows = consts.tile([P, D], BF16)
+        nc.vector.memset(bias_rows[:], 0.0)
+        nc.sync.dma_start(out=bias_rows[0:1, :], in_=bv.rearrange("(o d) -> o d", o=1))
+        q_raw = [load_rows(q_proj[0], "(p r) d -> p r d", "q_raw")]
+        val_raw = [load_rows(values[0], "(c p) d -> p c d", "val_raw")]
+        wv_raw = consts.tile([P, PASSES, PACK, D], BF16)
+        nc.sync.dma_start(
+            out=wv_raw[:].rearrange("p g t n -> p g (t n)"),
+            in_=Wv.rearrange("(g p t) n -> p g (t n)", p=P, t=PACK),
+        )
+        k_raw.append(load_rows(k_proj[1], "(c p) d -> p c d", "k_raw"))
+        q_raw.append(load_rows(q_proj[1], "(p r) d -> p r d", "q_raw"))
+        val_raw.append(load_rows(values[1], "(c p) d -> p c d", "val_raw"))
+
+        warm = consts.tile([P, 1], F32)
+        nc.vector.memset(warm[:], 0.0)
+        nc.scalar.activation(out=warm[:], in_=warm[:], func=ACT.Exp)
+        identity = consts.tile([P, P], F32)
+        make_identity(nc, identity[:])
+        ones = consts.tile([P, P], BF16)
+        nc.vector.memset(ones[:], 1.0)
+        stride_hits = consts.tile([P, TILES], F32)
+        for r in range(TILES):
+            hits = sum(1 for stride in STRIDES if r % stride == 0)
+            nc.vector.memset(stride_hits[:, r : r + 1], float(hits))
+        hits_per_stride = consts.tile([P, TILES], F32)
+        nc.vector.tensor_scalar_mul(out=hits_per_stride[:], in0=stride_hits[:], scalar1=1.0 / len(STRIDES))
+        bias_all = consts.tile([P, D], F32)
+        wv_codes = consts.tile([P, PASSES, D], U32, align_bytes=64)
+        wv_scales = consts.tile([P, PASSES, D], U8, align_bytes=64)
+
+        def new_operand(tag):
+            codes = mx.tile([P, S], U32, tag=tag + "_codes", align_bytes=64)
+            scales = mx.tile([P, S], U8, tag=tag + "_scales", align_bytes=64)
+            return codes, scales
+
+        def turn_bank(rows, half, pair):
+            words = rows[:].bitcast(F32)
+            turned = psum_two.tile([P, 2, 2, P], F32, tag="turned")
+            for i in range(2):
+                for u in range(2):
+                    first = (K_PASS // 2) * half
+                    nc.tensor.transpose(
+                        turned[:, i, u, :],
+                        words[:, 2 * pair + i, first + u : first + K_PASS // 2 : 2],
+                        identity[:],
+                    )
+            grouped = stage.tile([P, 2 * P, PACK], BF16, tag="grouped", bufs=6, align_bytes=64)
+            nc.scalar.copy(
+                out=grouped[:].bitcast(F32).rearrange("p (i r) u -> p i r u", i=2),
+                in_=turned[:].rearrange("p i u r -> p i r u"),
+            )
+            return grouped
+
+        def quantise_bank(grouped, operand, pair):
+            codes, scales = operand
+            cols = slice(2 * P * pair, 2 * P * (pair + 1))
+            nc.vector.quantize_mx(
+                out=codes[:, cols].bitcast(FP8X4),
+                scales=scales[:, cols],
+                in_=grouped[:].rearrange("p s t -> p (s t)"),
+            )
+
+        def regroup_wv(g, h):
+            wv_grouped = stage.tile([P, E, PACK], BF16, tag="wv_grouped", align_bytes=64)
+            nc.vector.tensor_copy(
+                out=wv_grouped[:].rearrange("p (c i) t -> p c t i", i=4),
+                in_=wv_raw[:, g, :, E * h : E * (h + 1)].rearrange("p t (c i) -> p c t i", i=4),
+            )
+            return wv_grouped
+
+        def quantise_wv(wv_grouped, g, h):
+            cols = slice(E * h, E * (h + 1))
+            nc.vector.quantize_mx(
+                out=wv_codes[:, g, cols].bitcast(FP8X4),
+                scales=wv_scales[:, g, cols],
+                in_=wv_grouped[:].rearrange("p n t -> p (n t)"),
+            )
+
+        def logit_matmuls(q_mx, k_mx, pair):
+            q_codes, q_scales = q_mx
+            k_codes, k_scales = k_mx
+            narrow = psum_one.tile([P, 2, REST], F32, tag="narrow")
+            wides = []
+            for i in range(2):
+                rows = slice(P * (2 * pair + i), P * (2 * pair + i + 1))
+                wide = psum_two.tile([P, BANK], F32, tag="wide")
+                wides.append(wide)
+                for target, cols in ((wide[:], slice(0, BANK)), (narrow[:, i, :], slice(BANK, S))):
+                    nc.tensor.matmul_mx(
+                        out=target,
+                        lhsT=q_codes[:, rows].bitcast(FP8X4),
+                        lhsT_scale=q_scales[:, rows],
+                        rhs=k_codes[:, cols].bitcast(FP8X4),
+                        rhs_scale=k_scales[:, cols],
+                        start=True,
+                        stop=True,
+                    )
+            return wides, narrow
+
+        def logits_out(wides, narrow):
+            logits = logit_pool.tile([P, 2, S], F32, tag="logits")
+            wide_max = small.tile([P, 2], F32, tag="wide_max")
+            row_max = small.tile([P, 2], F32, tag="row_max")
+            for i in range(2):
+                nc.vector.tensor_scalar(
+                    out=logits[:, i, 0:BANK], in0=wides[i][:], scalar1=1.0, scalar2=None,
+                    op0=ALU.mult, op1=ALU.max, accum_out=wide_max[:, i : i + 1],
+                )
+            for i in range(2):
+                nc.vector.tensor_scalar(
+                    out=logits[:, i, BANK:S], in0=narrow[:, i, :], scalar1=1.0,
+                    scalar2=wide_max[:, i : i + 1],
+                    op0=ALU.mult, op1=ALU.max, accum_out=row_max[:, i : i + 1],
+                )
+            neg_max = small.tile([P, 2], F32, tag="neg_max")
+            nc.vector.tensor_scalar_mul(out=neg_max[:], in0=row_max[:], scalar1=-1.0)
+            return logits, neg_max
+
+        def store_logits(b, h, pair, logits):
+            nc.sync.dma_start(
+                out=out_1[b, h].rearrange("(a r) s -> a r s", r=TILES)[:, 2 * pair : 2 * pair + 2, :],
+                in_=logits[:],
+            )
+            for stride in STRIDES[1:]:
+                for i in range(2):
+                    r = 2 * pair + i
+                    if r % stride == 0:
+                        nc.sync.dma_start(
+                            out=attn_out[stride][b, h].rearrange("(a m) s -> a m s", m=TILES // stride)[
+                                :, r // stride, :
+                            ],
+                            in_=logits[:, i, :],
+                        )
+
+        def exponentials(logits, neg_max):
+            row_sum = small.tile([P, 2], F32, tag="row_sum")
+            expos = []
+            for i in range(2):
+                expo = expo_pool.tile([P, S], F32, tag="expo")
+                expos.append(expo)
+                nc.scalar.activation(
+                    out=expo[:], in_=logits[:, i, :], func=ACT.Exp,
+                    bias=neg_max[:, i : i + 1], scale=1.0, accum_out=row_sum[:, i : i + 1],
+                )
+            return expos, row_sum
+
+        def high_halves(expo):
+            return expo[:].bitcast(BF16).rearrange("p (s half) -> p s half", half=2)[:, :, 1]
+
+        def low_parts(expos):
+            lows = []
+            for expo in expos:
+                low = low_pool.tile([P, S], BF16, tag="low")
+                lows.append(low)
+                nc.gpsimd.tensor_tensor(out=low[:], in0=expo[:], in1=high_halves(expo), op=ALU.subtract)
+            return lows
+
+        def row_weights(row_sum, pair):
+            inv_sum = small.tile([P, 2], F32, tag="inv_sum")
+            nc.vector.reciprocal(out=inv_sum[:], in_=row_sum[:])
+            weight = small.tile([P, 2], F32, tag="weight")
+            nc.gpsimd.tensor_tensor(
+                out=weight[:], in0=inv_sum[:], in1=hits_per_stride[:, 2 * pair : 2 * pair + 2], op=ALU.mult
+            )
+            repeated = weight[:].unsqueeze(2).to_broadcast([P, 2, REPEAT])
+            pieces = small.tile([P, 2, 2, REPEAT], BF16, tag="pieces")
+            nc.gpsimd.tensor_scalar(
+                out=pieces[:, :, 0, :], in0=repeated, scalar1=1.0, scalar2=0.0, op0=ALU.mult, op1=ALU.add
+            )
+            nc.gpsimd.tensor_tensor(out=pieces[:, :, 1, :], in0=repeated, in1=pieces[:, :, 0, :], op=ALU.subtract)
+            return pieces
+
+        def column_sums(partial, pair, expos, lows, pieces):
+            for c in range(TILES):
+                chunk = slice(P * c, P * (c + 1))
+                for i in range(2):
+                    for part, stationary in enumerate((high_halves(expos[i])[:, chunk], lows[i][:, chunk])):
+                        nc.tensor.matmul(
+                            out=partial[:, c, pair].rearrange("p w r -> p (w r)"),
+                            lhsT=stationary,
+                            rhs=pieces[:, i].rearrange("p w r -> p (w r)"),
+                            start=(i == 0 and part == 0),
+                            stop=(i == 1 and part == 1),
+                        )
+
+        def close_head(partial, head):
+            col_sums[head] = small.tile([P, TILES], F32, name="col_sum", tag="col_sum")
+            nc.vector.tensor_reduce(
+                out=col_sums[head][:], in_=partial[:, :, :, :, 0], axis=mybir.AxisListType.XY, op=ALU.add
+            )
+
+        def value_matmuls(b, h, pair):
+            products = []
+            for c in (2 * pair, 2 * pair + 1):
+                rows = slice(P * c, P * (c + 1))
+                cols = slice(E * h, E * (h + 1))
+                acc = psum_two.tile([P, BANK], F32, tag="acc")
+                for g in range(PASSES):
+                    val_codes, val_scales = operands[("val", b, g)]
+                    nc.tensor.matmul_mx(
+                        out=acc[:],
+                        lhsT=val_codes[:, rows].bitcast(FP8X4),
+                        lhsT_scale=val_scales[:, rows],
+                        rhs=wv_codes[:, g, cols].bitcast(FP8X4),
+                        rhs_scale=wv_scales[:, g, cols],
+                        start=(g == 0),
+                        stop=(g == PASSES - 1),
+                    )
+                products.append((acc, b, h, c))
+            return products
+
+        def add_bias(products):
+            biased = []
+            for acc, b, h, c in products:
+                gated = gated_pool.tile([P, E], F32, tag="gated")
+                nc.vector.tensor_tensor(
+                    out=gated[:], in0=acc[:], in1=bias_all[:, E * h : E * (h + 1)], op=ALU.add
+                )
+                biased.append((gated, b, h, c))
+            return biased
+
+        def gate_and_store(biased, share_with_vector=False):
+            for gated, b, h, c in biased:
+                gate = col_sums[(b, h)][:, c : c + 1]
+                if share_with_vector and c % 2 == 1:
+                    nc.vector.tensor_scalar_mul(out=gated[:], in0=gated[:], scalar1=gate)
+                else:
+                    nc.scalar.activation(out=gated[:], in_=gated[:], func=ACT.Copy, scale=gate)
+                nc.sync.dma_start(
+                    out=out_0[b, P * c : P * (c + 1), E * h : E * (h + 1)], in_=gated[:]
+                )
+
+        operands = {}
+        col_sums = {}
+        sources = {"k": k_raw, "q": q_raw, "val": val_raw}
+
+        def operands_prepared_during(b, h):
+            if h + 1 < H:
+                return [("k", b, h + 1), ("q", b, h + 1)] + [("val", b, g) for g in range(PASSES)]
+            if b + 1 < B:
+                return [("k", b + 1, 0), ("q", b + 1, 0)]
+            return []
+
+        def operand_tag(key):
+            return key[0] if key[0] != "val" else "val%d" % key[2]
+
+        for key in (("k", 0, 0), ("q", 0, 0)):
+            operands[key] = new_operand(operand_tag(key))
+            for pair in range(PAIRS):
+                quantise_bank(turn_bank(sources[key[0]][0], 0, pair), operands[key], pair)
+            if key[0] == "k":
+                for h in range(H):
+                    cols = slice(E * h, E * (h + 1))
+                    spread = psum_two.tile([P, BANK], F32, tag="acc")
+                    nc.tensor.matmul(
+                        out=spread[:], lhsT=ones[:], rhs=bias_rows[:, cols], start=True, stop=True
+                    )
+                    nc.vector.tensor_copy(out=bias_all[:, cols], in_=spread[:])
+
+        lagging = None
+        partial = None
+        closing = None
+        products = []
+        biased = []
+        gated_head = None
+        for b in range(B):
+            for h in range(H):
+                coming = operands_prepared_during(b, h)
+                for key in coming:
+                    operands[key] = new_operand(operand_tag(key))
+                for pair in range(PAIRS):
+                    gate_and_store(biased)
+                    if closing is not None:
+                        close_head(partial, closing)
+                        closing = None
+                    biased = add_bias(products)
+                    if lagging is not None:
+                        pieces = row_weights(lagging[4], lagging[2])
+                    wides, narrow = logit_matmuls(operands[("q", b, h)], operands[("k", b, h)], pair)
+                    logits, neg_max = logits_out(wides, narrow)
+                    store_logits(b, h, pair, logits)
+                    turned_banks = [turn_bank(sources[key[0]][key[1]], key[2], pair) for key in coming]
+                    products = value_matmuls(gated_head[0], gated_head[1], pair) if gated_head else []
+                    if lagging is not None:
+                        if lagging[2] == 0:
+                            partial = psum_one.tile([P, TILES, PAIRS, 2, REPEAT], F32, tag="partial")
+                        column_sums(partial, lagging[2], lagging[3], lagging[5], pieces)
+                        if lagging[2] == PAIRS - 1:
+                            closing = (lagging[0], lagging[1])
+                    wv_pass = pair - 1
+                    if b == 0 and wv_pass >= 0:
+                        wv_grouped = regroup_wv(wv_pass, h)
+                    for key, grouped in zip(coming, turned_banks):
+                        quantise_bank(grouped, operands[key], pair)
+                    if b == 0 and wv_pass >= 0:
+                        quantise_wv(wv_grouped, wv_pass, h)
+                    expos, row_sum = exponentials(logits, neg_max)
+                    lagging = (b, h, pair, expos, row_sum, low_parts(expos))
+                gated_head = (b, h)
+
+        gate_and_store(biased)
+        gate_and_store(add_bias(products))
+        pieces = row_weights(lagging[4], lagging[2])
+        biased = []
+        for pair in range(PAIRS):
+            biased.extend(add_bias(value_matmuls(gated_head[0], gated_head[1], pair)))
+        column_sums(partial, lagging[2], lagging[3], lagging[5], pieces)
+        close_head(partial, gated_head)
+        gate_and_store(biased, share_with_vector=True)

@@ -42,37 +42,54 @@ def tile_trendattentionlayer_pa_kernel(
         raw = ctx.enter_context(tc.tile_pool(name="raw", bufs=B))
         stage = ctx.enter_context(tc.tile_pool(name="stage", bufs=2))
         mx = ctx.enter_context(tc.tile_pool(name="mx", bufs=2))
-        logit_pool = ctx.enter_context(tc.tile_pool(name="logit_pool", bufs=6))
+        logit_pool = ctx.enter_context(tc.tile_pool(name="logit_pool", bufs=5))
         expo_pool = ctx.enter_context(tc.tile_pool(name="expo_pool", bufs=4))
         low_pool = ctx.enter_context(tc.tile_pool(name="low_pool", bufs=4))
-        gated_pool = ctx.enter_context(tc.tile_pool(name="gated_pool", bufs=10))
+        gated_pool = ctx.enter_context(tc.tile_pool(name="gated_pool", bufs=12))
         small = ctx.enter_context(tc.tile_pool(name="small", bufs=4))
         psum_two = ctx.enter_context(tc.psum_pool(name="psum_two", bufs=2))
+        psum_flex = ctx.enter_context(tc.psum_pool(name="psum_flex", bufs=4))
         psum_one = ctx.enter_context(tc.psum_pool(name="psum_one", bufs=1))
         ctx.enter_context(tc.manual_schedule())
 
-        def load_rows(source, pattern, tag):
-            rows = raw.tile([P, TILES, D], BF16, tag=tag)
-            view = source.rearrange(pattern, p=P)
-            for pair in range(PAIRS):
-                piece = slice(2 * pair, 2 * pair + 2)
-                nc.sync.dma_start(out=rows[:, piece, :], in_=view[:, piece, :])
-            return rows
+        views = {}
+        raws = {}
+        for b in range(B):
+            for name, source, pattern in (
+                ("k", k_proj, "(c p) d -> p c d"),
+                ("q", q_proj, "(p r) d -> p r d"),
+                ("val", values, "(c p) d -> p c d"),
+            ):
+                views[(name, b)] = source[b].rearrange(pattern, p=P)
+                rows = raw.tile([P, TILES, D], BF16, name=name + "_raw", tag=name + "_raw")
+                raws[(name, b)] = rows
 
-        k_raw = [load_rows(k_proj[0], "(c p) d -> p c d", "k_raw")]
+        def load(name, b, tiles, cols):
+            nc.sync.dma_start(out=raws[(name, b)][:, tiles, cols], in_=views[(name, b)][:, tiles, cols])
+
+        def pair_slice(pair):
+            return slice(2 * pair, 2 * pair + 2)
+
+        everything = slice(0, TILES)
+        for name in ("k", "q"):
+            for pair in range(PAIRS):
+                load(name, 0, pair_slice(pair), slice(0, E))
         bias_rows = consts.tile([P, D], BF16)
         nc.vector.memset(bias_rows[:], 0.0)
         nc.sync.dma_start(out=bias_rows[0:1, :], in_=bv.rearrange("(o d) -> o d", o=1))
-        q_raw = [load_rows(q_proj[0], "(p r) d -> p r d", "q_raw")]
-        val_raw = [load_rows(values[0], "(c p) d -> p c d", "val_raw")]
+        load("k", 0, everything, slice(E, D))
+        load("q", 0, everything, slice(E, D))
         wv_raw = consts.tile([P, PASSES, PACK, D], BF16)
-        nc.sync.dma_start(
-            out=wv_raw[:].rearrange("p g t n -> p g (t n)"),
-            in_=Wv.rearrange("(g p t) n -> p g (t n)", p=P, t=PACK),
-        )
-        k_raw.append(load_rows(k_proj[1], "(c p) d -> p c d", "k_raw"))
-        q_raw.append(load_rows(q_proj[1], "(p r) d -> p r d", "q_raw"))
-        val_raw.append(load_rows(values[1], "(c p) d -> p c d", "val_raw"))
+        for g in range(PASSES):
+            nc.sync.dma_start(
+                out=wv_raw[:, g].rearrange("p t n -> p (t n)"),
+                in_=Wv[K_PASS * g : K_PASS * (g + 1), :].rearrange("(p t) n -> p (t n)", t=PACK),
+            )
+        for pair in range(PAIRS):
+            load("val", 0, pair_slice(pair), slice(0, D))
+        for name in ("k", "q", "val"):
+            for pair in range(PAIRS):
+                load(name, 1, pair_slice(pair), slice(0, D))
 
         warm = consts.tile([P, 1], F32)
         nc.vector.memset(warm[:], 0.0)
@@ -91,14 +108,21 @@ def tile_trendattentionlayer_pa_kernel(
         wv_codes = consts.tile([P, PASSES, D], U32, align_bytes=64)
         wv_scales = consts.tile([P, PASSES, D], U8, align_bytes=64)
 
-        def new_operand(tag):
-            codes = mx.tile([P, S], U32, tag=tag + "_codes", align_bytes=64)
-            scales = mx.tile([P, S], U8, tag=tag + "_scales", align_bytes=64)
-            return codes, scales
+        operands = {}
 
-        def turn_bank(rows, half, pair):
-            words = rows[:].bitcast(F32)
-            turned = psum_two.tile([P, 2, 2, P], F32, tag="turned")
+        def operand(name, b, half):
+            key = (name, b, half)
+            if key not in operands:
+                tag = name if name != "val" else "val%d" % half
+                codes = mx.tile([P, S], U32, name="codes", tag=tag + "_codes", align_bytes=64)
+                scales = mx.tile([P, S], U8, name="scales", tag=tag + "_scales", align_bytes=64)
+                operands[key] = (codes, scales)
+            return operands[key]
+
+        def turn(bank):
+            name, b, half, pair = bank
+            words = raws[(name, b)][:].bitcast(F32)
+            turned = psum_flex.tile([P, 2, 2, P], F32, name="turned", tag="flex")
             for i in range(2):
                 for u in range(2):
                     first = (K_PASS // 2) * half
@@ -107,63 +131,66 @@ def tile_trendattentionlayer_pa_kernel(
                         words[:, 2 * pair + i, first + u : first + K_PASS // 2 : 2],
                         identity[:],
                     )
-            grouped = stage.tile([P, 2 * P, PACK], BF16, tag="grouped", bufs=6, align_bytes=64)
-            nc.scalar.copy(
-                out=grouped[:].bitcast(F32).rearrange("p (i r) u -> p i r u", i=2),
-                in_=turned[:].rearrange("p i u r -> p i r u"),
-            )
+            return turned
+
+        def gather_words(turned, on_vector=False):
+            grouped = stage.tile([P, 2 * P, PACK], BF16, name="grouped", tag="grouped", bufs=6, align_bytes=64)
+            out = grouped[:].bitcast(F32).rearrange("p (i r) u -> p i r u", i=2)
+            source = turned[:].rearrange("p i u r -> p i r u")
+            if on_vector:
+                nc.vector.tensor_copy(out=out, in_=source)
+            else:
+                nc.scalar.copy(out=out, in_=source)
             return grouped
 
-        def quantise_bank(grouped, operand, pair):
-            codes, scales = operand
+        def quantise(grouped, bank):
+            name, b, half, pair = bank
+            codes, scales = operand(name, b, half)
             cols = slice(2 * P * pair, 2 * P * (pair + 1))
             nc.vector.quantize_mx(
-                out=codes[:, cols].bitcast(FP8X4),
-                scales=scales[:, cols],
+                out=codes[:, cols].bitcast(FP8X4), scales=scales[:, cols],
                 in_=grouped[:].rearrange("p s t -> p (s t)"),
             )
 
-        def regroup_wv(g, h):
-            wv_grouped = stage.tile([P, E, PACK], BF16, tag="wv_grouped", align_bytes=64)
-            nc.vector.tensor_copy(
-                out=wv_grouped[:].rearrange("p (c i) t -> p c t i", i=4),
-                in_=wv_raw[:, g, :, E * h : E * (h + 1)].rearrange("p t (c i) -> p c t i", i=4),
-            )
+        def regroup_wv(g, h, engine):
+            wv_grouped = stage.tile([P, E, PACK], BF16, name="wv_grouped", tag="wv_grouped", align_bytes=64)
+            out = wv_grouped[:].rearrange("p (c i) t -> p c t i", i=4)
+            source = wv_raw[:, g, :, E * h : E * (h + 1)].rearrange("p t (c i) -> p c t i", i=4)
+            if engine == "S":
+                nc.scalar.copy(out=out, in_=source)
+            else:
+                nc.vector.tensor_copy(out=out, in_=source)
             return wv_grouped
 
         def quantise_wv(wv_grouped, g, h):
             cols = slice(E * h, E * (h + 1))
             nc.vector.quantize_mx(
-                out=wv_codes[:, g, cols].bitcast(FP8X4),
-                scales=wv_scales[:, g, cols],
+                out=wv_codes[:, g, cols].bitcast(FP8X4), scales=wv_scales[:, g, cols],
                 in_=wv_grouped[:].rearrange("p n t -> p (n t)"),
             )
 
-        def logit_matmuls(q_mx, k_mx, pair):
-            q_codes, q_scales = q_mx
-            k_codes, k_scales = k_mx
-            narrow = psum_one.tile([P, 2, REST], F32, tag="narrow")
+        def logit_matmuls(b, h, pair):
+            q_codes, q_scales = operand("q", b, h)
+            k_codes, k_scales = operand("k", b, h)
+            narrow = psum_one.tile([P, 2, REST], F32, name="narrow", tag="narrow")
             wides = []
             for i in range(2):
                 rows = slice(P * (2 * pair + i), P * (2 * pair + i + 1))
-                wide = psum_two.tile([P, BANK], F32, tag="wide")
+                wide = psum_two.tile([P, BANK], F32, name="wide", tag="wide")
                 wides.append(wide)
                 for target, cols in ((wide[:], slice(0, BANK)), (narrow[:, i, :], slice(BANK, S))):
                     nc.tensor.matmul_mx(
                         out=target,
-                        lhsT=q_codes[:, rows].bitcast(FP8X4),
-                        lhsT_scale=q_scales[:, rows],
-                        rhs=k_codes[:, cols].bitcast(FP8X4),
-                        rhs_scale=k_scales[:, cols],
-                        start=True,
-                        stop=True,
+                        lhsT=q_codes[:, rows].bitcast(FP8X4), lhsT_scale=q_scales[:, rows],
+                        rhs=k_codes[:, cols].bitcast(FP8X4), rhs_scale=k_scales[:, cols],
+                        start=True, stop=True,
                     )
             return wides, narrow
 
         def logits_out(wides, narrow):
-            logits = logit_pool.tile([P, 2, S], F32, tag="logits")
-            wide_max = small.tile([P, 2], F32, tag="wide_max")
-            row_max = small.tile([P, 2], F32, tag="row_max")
+            logits = logit_pool.tile([P, 2, S], F32, name="logits", tag="logits")
+            wide_max = small.tile([P, 2], F32, name="wide_max", tag="wide_max")
+            row_max = small.tile([P, 2], F32, name="row_max", tag="row_max")
             for i in range(2):
                 nc.vector.tensor_scalar(
                     out=logits[:, i, 0:BANK], in0=wides[i][:], scalar1=1.0, scalar2=None,
@@ -175,9 +202,7 @@ def tile_trendattentionlayer_pa_kernel(
                     scalar2=wide_max[:, i : i + 1],
                     op0=ALU.mult, op1=ALU.max, accum_out=row_max[:, i : i + 1],
                 )
-            neg_max = small.tile([P, 2], F32, tag="neg_max")
-            nc.vector.tensor_scalar_mul(out=neg_max[:], in0=row_max[:], scalar1=-1.0)
-            return logits, neg_max
+            return logits, row_max
 
         def store_logits(b, h, pair, logits):
             nc.sync.dma_start(
@@ -195,11 +220,16 @@ def tile_trendattentionlayer_pa_kernel(
                             in_=logits[:, i, :],
                         )
 
+        def negate(row_max):
+            neg_max = small.tile([P, 2], F32, name="neg_max", tag="neg_max")
+            nc.vector.tensor_scalar_mul(out=neg_max[:], in0=row_max[:], scalar1=-1.0)
+            return neg_max
+
         def exponentials(logits, neg_max):
-            row_sum = small.tile([P, 2], F32, tag="row_sum")
+            row_sum = small.tile([P, 2], F32, name="row_sum", tag="row_sum")
             expos = []
             for i in range(2):
-                expo = expo_pool.tile([P, S], F32, tag="expo")
+                expo = expo_pool.tile([P, S], F32, name="expo", tag="expo")
                 expos.append(expo)
                 nc.scalar.activation(
                     out=expo[:], in_=logits[:, i, :], func=ACT.Exp,
@@ -213,20 +243,20 @@ def tile_trendattentionlayer_pa_kernel(
         def low_parts(expos):
             lows = []
             for expo in expos:
-                low = low_pool.tile([P, S], BF16, tag="low")
+                low = low_pool.tile([P, S], BF16, name="low", tag="low")
                 lows.append(low)
                 nc.gpsimd.tensor_tensor(out=low[:], in0=expo[:], in1=high_halves(expo), op=ALU.subtract)
             return lows
 
         def row_weights(row_sum, pair):
-            inv_sum = small.tile([P, 2], F32, tag="inv_sum")
+            inv_sum = small.tile([P, 2], F32, name="inv_sum", tag="inv_sum")
             nc.vector.reciprocal(out=inv_sum[:], in_=row_sum[:])
-            weight = small.tile([P, 2], F32, tag="weight")
+            weight = small.tile([P, 2], F32, name="weight", tag="weight")
             nc.gpsimd.tensor_tensor(
                 out=weight[:], in0=inv_sum[:], in1=hits_per_stride[:, 2 * pair : 2 * pair + 2], op=ALU.mult
             )
             repeated = weight[:].unsqueeze(2).to_broadcast([P, 2, REPEAT])
-            pieces = small.tile([P, 2, 2, REPEAT], BF16, tag="pieces")
+            pieces = small.tile([P, 2, 2, REPEAT], BF16, name="pieces", tag="pieces")
             nc.gpsimd.tensor_scalar(
                 out=pieces[:, :, 0, :], in0=repeated, scalar1=1.0, scalar2=0.0, op0=ALU.mult, op1=ALU.add
             )
@@ -242,131 +272,134 @@ def tile_trendattentionlayer_pa_kernel(
                             out=partial[:, c, pair].rearrange("p w r -> p (w r)"),
                             lhsT=stationary,
                             rhs=pieces[:, i].rearrange("p w r -> p (w r)"),
-                            start=(i == 0 and part == 0),
-                            stop=(i == 1 and part == 1),
+                            start=(i == 0 and part == 0), stop=(i == 1 and part == 1),
                         )
 
-        def close_head(partial, head):
-            col_sums[head] = small.tile([P, TILES], F32, name="col_sum", tag="col_sum")
+        def close_head(key, partial):
+            col_sum = small.tile([P, TILES], F32, name="col_sum", tag="col_sum")
             nc.vector.tensor_reduce(
-                out=col_sums[head][:], in_=partial[:, :, :, :, 0], axis=mybir.AxisListType.XY, op=ALU.add
+                out=col_sum[:], in_=partial[:, :, :, :, 0], axis=mybir.AxisListType.XY, op=ALU.add
             )
+            gates[key] = col_sum
 
-        def value_matmuls(b, h, pair):
-            products = []
-            for c in (2 * pair, 2 * pair + 1):
-                rows = slice(P * c, P * (c + 1))
-                cols = slice(E * h, E * (h + 1))
-                acc = psum_two.tile([P, BANK], F32, tag="acc")
-                for g in range(PASSES):
-                    val_codes, val_scales = operands[("val", b, g)]
-                    nc.tensor.matmul_mx(
-                        out=acc[:],
-                        lhsT=val_codes[:, rows].bitcast(FP8X4),
-                        lhsT_scale=val_scales[:, rows],
-                        rhs=wv_codes[:, g, cols].bitcast(FP8X4),
-                        rhs_scale=wv_scales[:, g, cols],
-                        start=(g == 0),
-                        stop=(g == PASSES - 1),
-                    )
-                products.append((acc, b, h, c))
-            return products
-
-        def add_bias(products):
-            biased = []
-            for acc, b, h, c in products:
-                gated = gated_pool.tile([P, E], F32, tag="gated")
-                nc.vector.tensor_tensor(
-                    out=gated[:], in0=acc[:], in1=bias_all[:, E * h : E * (h + 1)], op=ALU.add
+        def value_matmul(b, h, c):
+            rows = slice(P * c, P * (c + 1))
+            cols = slice(E * h, E * (h + 1))
+            acc = psum_flex.tile([P, BANK], F32, name="acc", tag="flex")
+            for g in range(PASSES):
+                val_codes, val_scales = operand("val", b, g)
+                nc.tensor.matmul_mx(
+                    out=acc[:],
+                    lhsT=val_codes[:, rows].bitcast(FP8X4), lhsT_scale=val_scales[:, rows],
+                    rhs=wv_codes[:, g, cols].bitcast(FP8X4), rhs_scale=wv_scales[:, g, cols],
+                    start=(g == 0), stop=(g == PASSES - 1),
                 )
-                biased.append((gated, b, h, c))
-            return biased
+            return acc
 
-        def gate_and_store(biased, share_with_vector=False):
-            for gated, b, h, c in biased:
-                gate = col_sums[(b, h)][:, c : c + 1]
-                if share_with_vector and c % 2 == 1:
-                    nc.vector.tensor_scalar_mul(out=gated[:], in0=gated[:], scalar1=gate)
-                else:
-                    nc.scalar.activation(out=gated[:], in_=gated[:], func=ACT.Copy, scale=gate)
-                nc.sync.dma_start(
-                    out=out_0[b, P * c : P * (c + 1), E * h : E * (h + 1)], in_=gated[:]
-                )
+        def add_bias(acc, h):
+            gated = gated_pool.tile([P, E], F32, name="gated", tag="gated")
+            nc.vector.tensor_tensor(
+                out=gated[:], in0=acc[:], in1=bias_all[:, E * h : E * (h + 1)], op=ALU.add
+            )
+            return gated
 
-        operands = {}
-        col_sums = {}
-        sources = {"k": k_raw, "q": q_raw, "val": val_raw}
+        def gate_and_store(gated, b, h, c, on_vector=False):
+            gate = gates[(b, h)][:, c : c + 1]
+            if on_vector:
+                nc.vector.tensor_scalar_mul(out=gated[:], in0=gated[:], scalar1=gate)
+            else:
+                nc.scalar.activation(out=gated[:], in_=gated[:], func=ACT.Copy, scale=gate)
+            nc.sync.dma_start(out=out_0[b, P * c : P * (c + 1), E * h : E * (h + 1)], in_=gated[:])
 
-        def operands_prepared_during(b, h):
-            if h + 1 < H:
-                return [("k", b, h + 1), ("q", b, h + 1)] + [("val", b, g) for g in range(PASSES)]
-            if b + 1 < B:
-                return [("k", b + 1, 0), ("q", b + 1, 0)]
-            return []
+        slots = [(b, h, pair) for b in range(B) for h in range(H) for pair in range(PAIRS)]
+        gates = {}
+        prep = {
+            0: [("q", 0, 0, 2), ("k", 0, 1, 0)],
+            1: [("k", 0, 1, 1), ("k", 0, 1, 2), ("q", 0, 1, 0)],
+            2: [("q", 0, 1, 1), ("val", 0, 0, 0), ("val", 0, 1, 0)],
+            3: [("q", 0, 1, 2), ("val", 0, 0, 1), ("val", 0, 1, 1), ("k", 1, 0, 0)],
+            4: [("k", 1, 0, 1), ("k", 1, 0, 2), ("q", 1, 0, 0)],
+            5: [("q", 1, 0, 1), ("val", 0, 0, 2), ("val", 0, 1, 2)],
+            6: [("q", 1, 0, 2), ("k", 1, 1, 0), ("val", 1, 0, 0), ("val", 1, 1, 0)],
+            7: [("k", 1, 1, 1), ("k", 1, 1, 2), ("q", 1, 1, 0)],
+            8: [("q", 1, 1, 1), ("val", 1, 0, 1), ("val", 1, 1, 1)],
+            9: [("q", 1, 1, 2), ("val", 1, 0, 2), ("val", 1, 1, 2)],
+            10: [], 11: [],
+        }
+        wv_plan = {1: [(0, 0, "V"), (1, 0, "S")], 2: [(0, 1, "S")], 3: [(1, 1, "S")]}
+        v_plan = {
+            4: [(0, 0, 0)], 5: [(0, 0, 1), (0, 1, 0)], 6: [(0, 1, 1)], 7: [(0, 0, 2), (0, 1, 2)],
+            8: [(1, 0, 0)], 9: [(1, 1, 0)], 10: [(1, 0, 1), (1, 1, 1)],
+            11: [(1, 0, 2), (1, 1, 2)],
+        }
+        first = [("k", 0, 0, pair) for pair in range(PAIRS)] + [("q", 0, 0, 0), ("q", 0, 0, 1)]
+        grouped = []
+        for j, bank in enumerate(first[:4]):
+            grouped.append(gather_words(turn(bank), on_vector=(j % 2 == 1)))
+            if j >= 1:
+                quantise(grouped[j - 1], first[j - 1])
+        quantise(grouped[-1], first[3])
+        wides, narrow = logit_matmuls(0, 0, 0)
+        pending = [(gather_words(turn(first[4])), first[4])]
 
-        def operand_tag(key):
-            return key[0] if key[0] != "val" else "val%d" % key[2]
-
-        for key in (("k", 0, 0), ("q", 0, 0)):
-            operands[key] = new_operand(operand_tag(key))
-            for pair in range(PAIRS):
-                quantise_bank(turn_bank(sources[key[0]][0], 0, pair), operands[key], pair)
-            if key[0] == "k":
-                for h in range(H):
-                    cols = slice(E * h, E * (h + 1))
-                    spread = psum_two.tile([P, BANK], F32, tag="acc")
-                    nc.tensor.matmul(
-                        out=spread[:], lhsT=ones[:], rhs=bias_rows[:, cols], start=True, stop=True
-                    )
-                    nc.vector.tensor_copy(out=bias_all[:, cols], in_=spread[:])
-
-        lagging = None
-        partial = None
+        waiting = []
+        before = None
         closing = None
-        products = []
-        biased = []
-        gated_head = None
-        for b in range(B):
-            for h in range(H):
-                coming = operands_prepared_during(b, h)
-                for key in coming:
-                    operands[key] = new_operand(operand_tag(key))
-                for pair in range(PAIRS):
-                    gate_and_store(biased)
-                    if closing is not None:
-                        close_head(partial, closing)
-                        closing = None
-                    biased = add_bias(products)
-                    if lagging is not None:
-                        pieces = row_weights(lagging[4], lagging[2])
-                    wides, narrow = logit_matmuls(operands[("q", b, h)], operands[("k", b, h)], pair)
-                    logits, neg_max = logits_out(wides, narrow)
-                    store_logits(b, h, pair, logits)
-                    turned_banks = [turn_bank(sources[key[0]][key[1]], key[2], pair) for key in coming]
-                    products = value_matmuls(gated_head[0], gated_head[1], pair) if gated_head else []
-                    if lagging is not None:
-                        if lagging[2] == 0:
-                            partial = psum_one.tile([P, TILES, PAIRS, 2, REPEAT], F32, tag="partial")
-                        column_sums(partial, lagging[2], lagging[3], lagging[5], pieces)
-                        if lagging[2] == PAIRS - 1:
-                            closing = (lagging[0], lagging[1])
-                    wv_pass = pair - 1
-                    if b == 0 and wv_pass >= 0:
-                        wv_grouped = regroup_wv(wv_pass, h)
-                    for key, grouped in zip(coming, turned_banks):
-                        quantise_bank(grouped, operands[key], pair)
-                    if b == 0 and wv_pass >= 0:
-                        quantise_wv(wv_grouped, wv_pass, h)
-                    expos, row_sum = exponentials(logits, neg_max)
-                    lagging = (b, h, pair, expos, row_sum, low_parts(expos))
-                gated_head = (b, h)
+        partial = None
+        wv_pending = []
+        for n, (b, h, pair) in enumerate(slots):
+            done = []
+            exits = [(vb, vh, c) for vb, vh, vp in v_plan.get(n, []) for c in (2 * vp, 2 * vp + 1)]
+            for bank in prep[n]:
+                done.append((gather_words(turn(bank)), bank))
+            accs = [value_matmul(*x) for x in exits]
+            logits, row_max = logits_out(wides, narrow)
+            if before is not None:
+                pieces = row_weights(before[4], before[2])
+            store_logits(b, h, pair, logits)
+            for j, (group, bank) in enumerate(pending):
+                if j == 1:
+                    neg_max = negate(row_max)
+                quantise(group, bank)
+            if len(pending) < 2:
+                neg_max = negate(row_max)
+            pending = done
+            for wv_grouped, g, hh in wv_pending:
+                quantise_wv(wv_grouped, g, hh)
+            if n + 1 < len(slots):
+                wides, narrow = logit_matmuls(*slots[n + 1])
+            expos, row_sum = exponentials(logits, neg_max)
+            if closing is not None:
+                close_head(closing, partial)
+                closing = None
+            lows = low_parts(expos)
+            if before is not None:
+                if before[2] == 0:
+                    partial = psum_one.tile([P, TILES, PAIRS, 2, REPEAT], F32, name="partial", tag="partial")
+                column_sums(partial, before[2], before[3], before[5], pieces)
+                if before[2] == PAIRS - 1:
+                    closing = before[:2]
+            for j, x in enumerate(exits):
+                waiting.append((add_bias(accs[j], x[1]),) + x)
+            if n == 0:
+                for hh in range(H):
+                    cols = slice(E * hh, E * (hh + 1))
+                    spread = psum_flex.tile([P, BANK], F32, name="acc", tag="flex")
+                    nc.tensor.matmul(out=spread[:], lhsT=ones[:], rhs=bias_rows[:, cols], start=True, stop=True)
+                    nc.vector.tensor_copy(out=bias_all[:, cols], in_=spread[:])
+            wv_pending = [(regroup_wv(g, hh, e), g, hh) for g, hh, e in wv_plan.get(n, [])]
+            ready = [w for w in waiting if w[1:3] in gates]
+            for w in ready[:4]:
+                gate_and_store(*w)
+                waiting.remove(w)
+            before = (b, h, pair, expos, row_sum, lows)
 
-        gate_and_store(biased)
-        gate_and_store(add_bias(products))
-        pieces = row_weights(lagging[4], lagging[2])
-        biased = []
-        for pair in range(PAIRS):
-            biased.extend(add_bias(value_matmuls(gated_head[0], gated_head[1], pair)))
-        column_sums(partial, lagging[2], lagging[3], lagging[5], pieces)
-        close_head(partial, gated_head)
-        gate_and_store(biased, share_with_vector=True)
+        pieces = row_weights(before[4], before[2])
+        ready = [w for w in waiting if w[1:3] in gates]
+        for w in ready:
+            gate_and_store(*w)
+            waiting.remove(w)
+        column_sums(partial, before[2], before[3], before[5], pieces)
+        close_head(before[:2], partial)
+        for j, w in enumerate(waiting):
+            gate_and_store(*w, on_vector=(j % 2 == 1))

@@ -39,57 +39,62 @@ def tile_trendattentionlayer_pa_kernel(
 
     with ExitStack() as ctx:
         consts = ctx.enter_context(tc.tile_pool(name="consts", bufs=1))
-        raw = ctx.enter_context(tc.tile_pool(name="raw", bufs=B))
+        raw = ctx.enter_context(tc.tile_pool(name="raw", bufs=1))
         stage = ctx.enter_context(tc.tile_pool(name="stage", bufs=2))
         mx = ctx.enter_context(tc.tile_pool(name="mx", bufs=2))
         logit_pool = ctx.enter_context(tc.tile_pool(name="logit_pool", bufs=5))
         expo_pool = ctx.enter_context(tc.tile_pool(name="expo_pool", bufs=4))
         low_pool = ctx.enter_context(tc.tile_pool(name="low_pool", bufs=4))
-        gated_pool = ctx.enter_context(tc.tile_pool(name="gated_pool", bufs=12))
+        gated_pool = ctx.enter_context(tc.tile_pool(name="gated_pool", bufs=14))
         small = ctx.enter_context(tc.tile_pool(name="small", bufs=4))
         psum_two = ctx.enter_context(tc.psum_pool(name="psum_two", bufs=2))
         psum_flex = ctx.enter_context(tc.psum_pool(name="psum_flex", bufs=4))
         psum_one = ctx.enter_context(tc.psum_pool(name="psum_one", bufs=1))
         ctx.enter_context(tc.manual_schedule())
 
-        views = {}
+        def view(name, b):
+            source, pattern = {
+                "k": (k_proj, "(c p) d -> p c d"),
+                "q": (q_proj, "(p r) d -> p r d"),
+                "val": (values, "(c p) d -> p c d"),
+            }[name]
+            return source[b].rearrange(pattern, p=P)
+
         raws = {}
-        for b in range(B):
-            for name, source, pattern in (
-                ("k", k_proj, "(c p) d -> p c d"),
-                ("q", q_proj, "(p r) d -> p r d"),
-                ("val", values, "(c p) d -> p c d"),
-            ):
-                views[(name, b)] = source[b].rearrange(pattern, p=P)
-                rows = raw.tile([P, TILES, D], BF16, name=name + "_raw", tag=name + "_raw")
-                raws[(name, b)] = rows
 
-        def load(name, b, tiles, cols):
-            nc.sync.dma_start(out=raws[(name, b)][:, tiles, cols], in_=views[(name, b)][:, tiles, cols])
+        def load(name, b, h, tiles, place=None):
+            if (name, b, h) not in raws:
+                rows = raw.tile([P, TILES, E], BF16, name=name + "_raw", tag=place or "%s_raw%d" % (name, h))
+                raws[(name, b, h)] = (rows, 0)
+            rows = raws[(name, b, h)][0]
+            nc.sync.dma_start(out=rows[:, tiles, :], in_=view(name, b)[:, tiles, E * h : E * (h + 1)])
 
-        def pair_slice(pair):
-            return slice(2 * pair, 2 * pair + 2)
+        def load_whole(name, b):
+            rows = raw.tile([P, TILES, D], BF16, name=name + "_raw", tag="%s_raw_all%d" % (name, b))
+            nc.sync.dma_start(out=rows[:], in_=view(name, b))
+            for half in range(D // E):
+                raws[(name, b, half)] = (rows, E * half)
 
-        everything = slice(0, TILES)
-        for name in ("k", "q"):
-            for pair in range(PAIRS):
-                load(name, 0, pair_slice(pair), slice(0, E))
+        for pair in range(PAIRS):
+            load("k", 0, 0, slice(2 * pair, 2 * pair + 2))
+        load("q", 0, 0, slice(0, 2))
+        load("q", 0, 0, slice(2, TILES))
         bias_rows = consts.tile([P, D], BF16)
         nc.vector.memset(bias_rows[:], 0.0)
         nc.sync.dma_start(out=bias_rows[0:1, :], in_=bv.rearrange("(o d) -> o d", o=1))
-        load("k", 0, everything, slice(E, D))
-        load("q", 0, everything, slice(E, D))
-        wv_raw = consts.tile([P, PASSES, PACK, D], BF16)
+        load("k", 0, 1, slice(0, TILES))
+        load("q", 0, 1, slice(0, TILES))
+        wv_raws = []
         for g in range(PASSES):
+            wv_raw = consts.tile([P, PACK, D], BF16, name="wv_raw", tag="wv_raw%d" % g)
+            wv_raws.append(wv_raw)
             nc.sync.dma_start(
-                out=wv_raw[:, g].rearrange("p t n -> p (t n)"),
+                out=wv_raw[:].rearrange("p t n -> p (t n)"),
                 in_=Wv[K_PASS * g : K_PASS * (g + 1), :].rearrange("(p t) n -> p (t n)", t=PACK),
             )
-        for pair in range(PAIRS):
-            load("val", 0, pair_slice(pair), slice(0, D))
-        for name in ("k", "q", "val"):
-            for pair in range(PAIRS):
-                load(name, 1, pair_slice(pair), slice(0, D))
+        load_whole("val", 0)
+        for name in ("k", "q"):
+            load_whole(name, 1)
 
         warm = consts.tile([P, 1], F32)
         nc.vector.memset(warm[:], 0.0)
@@ -121,11 +126,12 @@ def tile_trendattentionlayer_pa_kernel(
 
         def turn(bank):
             name, b, half, pair = bank
-            words = raws[(name, b)][:].bitcast(F32)
+            rows, feature = raws[(name, b, half)]
+            words = rows[:].bitcast(F32)
             turned = psum_flex.tile([P, 2, 2, P], F32, name="turned", tag="flex")
             for i in range(2):
                 for u in range(2):
-                    first = (K_PASS // 2) * half
+                    first = feature // 2
                     nc.tensor.transpose(
                         turned[:, i, u, :],
                         words[:, 2 * pair + i, first + u : first + K_PASS // 2 : 2],
@@ -134,7 +140,7 @@ def tile_trendattentionlayer_pa_kernel(
             return turned
 
         def gather_words(turned, on_vector=False):
-            grouped = stage.tile([P, 2 * P, PACK], BF16, name="grouped", tag="grouped", bufs=6, align_bytes=64)
+            grouped = stage.tile([P, 2 * P, PACK], BF16, name="grouped", tag="grouped", bufs=8, align_bytes=64)
             out = grouped[:].bitcast(F32).rearrange("p (i r) u -> p i r u", i=2)
             source = turned[:].rearrange("p i u r -> p i r u")
             if on_vector:
@@ -155,7 +161,7 @@ def tile_trendattentionlayer_pa_kernel(
         def regroup_wv(g, h, engine):
             wv_grouped = stage.tile([P, E, PACK], BF16, name="wv_grouped", tag="wv_grouped", align_bytes=64)
             out = wv_grouped[:].rearrange("p (c i) t -> p c t i", i=4)
-            source = wv_raw[:, g, :, E * h : E * (h + 1)].rearrange("p t (c i) -> p c t i", i=4)
+            source = wv_raws[g][:, :, E * h : E * (h + 1)].rearrange("p t (c i) -> p c t i", i=4)
             if engine == "S":
                 nc.scalar.copy(out=out, in_=source)
             else:
@@ -222,7 +228,7 @@ def tile_trendattentionlayer_pa_kernel(
 
         def negate(row_max):
             neg_max = small.tile([P, 2], F32, name="neg_max", tag="neg_max")
-            nc.vector.tensor_scalar_mul(out=neg_max[:], in0=row_max[:], scalar1=-1.0)
+            nc.scalar.activation(out=neg_max[:], in_=row_max[:], func=ACT.Copy, scale=-1.0)
             return neg_max
 
         def exponentials(logits, neg_max):
@@ -240,12 +246,12 @@ def tile_trendattentionlayer_pa_kernel(
         def high_halves(expo):
             return expo[:].bitcast(BF16).rearrange("p (s half) -> p s half", half=2)[:, :, 1]
 
-        def low_parts(expos):
+        def low_parts(expos, engine):
             lows = []
             for expo in expos:
                 low = low_pool.tile([P, S], BF16, name="low", tag="low")
                 lows.append(low)
-                nc.gpsimd.tensor_tensor(out=low[:], in0=expo[:], in1=high_halves(expo), op=ALU.subtract)
+                engine.tensor_tensor(out=low[:], in0=expo[:], in1=high_halves(expo), op=ALU.subtract)
             return lows
 
         def row_weights(row_sum, pair):
@@ -316,21 +322,19 @@ def tile_trendattentionlayer_pa_kernel(
         prep = {
             0: [("q", 0, 0, 2), ("k", 0, 1, 0)],
             1: [("k", 0, 1, 1), ("k", 0, 1, 2), ("q", 0, 1, 0)],
-            2: [("q", 0, 1, 1), ("val", 0, 0, 0), ("val", 0, 1, 0)],
-            3: [("q", 0, 1, 2), ("val", 0, 0, 1), ("val", 0, 1, 1), ("k", 1, 0, 0)],
-            4: [("k", 1, 0, 1), ("k", 1, 0, 2), ("q", 1, 0, 0)],
-            5: [("q", 1, 0, 1), ("val", 0, 0, 2), ("val", 0, 1, 2)],
-            6: [("q", 1, 0, 2), ("k", 1, 1, 0), ("val", 1, 0, 0), ("val", 1, 1, 0)],
-            7: [("k", 1, 1, 1), ("k", 1, 1, 2), ("q", 1, 1, 0)],
-            8: [("q", 1, 1, 1), ("val", 1, 0, 1), ("val", 1, 1, 1)],
-            9: [("q", 1, 1, 2), ("val", 1, 0, 2), ("val", 1, 1, 2)],
-            10: [], 11: [],
+            2: [("q", 0, 1, 1), ("q", 0, 1, 2), ("val", 0, 0, 0), ("val", 0, 1, 0)],
+            3: [("k", 1, 0, 0), ("k", 1, 0, 1), ("val", 0, 0, 1), ("val", 0, 1, 1)],
+            4: [("k", 1, 0, 2), ("q", 1, 0, 0), ("val", 0, 0, 2), ("val", 0, 1, 2)],
+            5: [("q", 1, 0, 1), ("q", 1, 0, 2), ("val", 1, 0, 0), ("val", 1, 1, 0)],
+            6: [("k", 1, 1, 0), ("k", 1, 1, 1), ("k", 1, 1, 2), ("q", 1, 1, 0)],
+            7: [("q", 1, 1, 1), ("val", 1, 0, 1), ("val", 1, 1, 1)],
+            8: [("q", 1, 1, 2), ("val", 1, 0, 2), ("val", 1, 1, 2)],
+            9: [], 10: [], 11: [],
         }
-        wv_plan = {1: [(0, 0, "V"), (1, 0, "S")], 2: [(0, 1, "S")], 3: [(1, 1, "S")]}
+        wv_plan = {1: [(0, 0, "S"), (1, 0, "S")], 2: [(0, 1, "S")], 3: [(1, 1, "S")]}
         v_plan = {
-            4: [(0, 0, 0)], 5: [(0, 0, 1), (0, 1, 0)], 6: [(0, 1, 1)], 7: [(0, 0, 2), (0, 1, 2)],
-            8: [(1, 0, 0)], 9: [(1, 1, 0)], 10: [(1, 0, 1), (1, 1, 1)],
-            11: [(1, 0, 2), (1, 1, 2)],
+            4: [(0, 0, 0)], 5: [(0, 0, 1), (0, 1, 0)], 6: [(0, 1, 1), (0, 0, 2)], 7: [(0, 1, 2), (1, 0, 0)],
+            8: [(1, 1, 0)], 9: [(1, 0, 1), (1, 1, 1)], 10: [(1, 0, 2), (1, 1, 2)],
         }
         first = [("k", 0, 0, pair) for pair in range(PAIRS)] + [("q", 0, 0, 0), ("q", 0, 0, 1)]
         grouped = []
@@ -352,17 +356,17 @@ def tile_trendattentionlayer_pa_kernel(
             exits = [(vb, vh, c) for vb, vh, vp in v_plan.get(n, []) for c in (2 * vp, 2 * vp + 1)]
             for bank in prep[n]:
                 done.append((gather_words(turn(bank)), bank))
+            if n == 0:
+                for half, place in enumerate(("k_raw0", "q_raw0")):
+                    load("val", 1, half, slice(0, TILES), place)
             accs = [value_matmul(*x) for x in exits]
             logits, row_max = logits_out(wides, narrow)
             if before is not None:
                 pieces = row_weights(before[4], before[2])
             store_logits(b, h, pair, logits)
-            for j, (group, bank) in enumerate(pending):
-                if j == 1:
-                    neg_max = negate(row_max)
+            neg_max = negate(row_max)
+            for group, bank in pending:
                 quantise(group, bank)
-            if len(pending) < 2:
-                neg_max = negate(row_max)
             pending = done
             for wv_grouped, g, hh in wv_pending:
                 quantise_wv(wv_grouped, g, hh)
@@ -372,7 +376,7 @@ def tile_trendattentionlayer_pa_kernel(
             if closing is not None:
                 close_head(closing, partial)
                 closing = None
-            lows = low_parts(expos)
+            lows = low_parts(expos, nc.gpsimd) if n + 1 < len(slots) else None
             if before is not None:
                 if before[2] == 0:
                     partial = psum_one.tile([P, TILES, PAIRS, 2, REPEAT], F32, name="partial", tag="partial")
@@ -394,12 +398,15 @@ def tile_trendattentionlayer_pa_kernel(
                 waiting.remove(w)
             before = (b, h, pair, expos, row_sum, lows)
 
+        expos = before[3]
+        lows = low_parts(expos[:1], nc.vector)
         pieces = row_weights(before[4], before[2])
+        lows = lows + low_parts(expos[1:], nc.vector)
         ready = [w for w in waiting if w[1:3] in gates]
         for w in ready:
             gate_and_store(*w)
             waiting.remove(w)
-        column_sums(partial, before[2], before[3], before[5], pieces)
+        column_sums(partial, before[2], expos, lows, pieces)
         close_head(before[:2], partial)
         for j, w in enumerate(waiting):
             gate_and_store(*w, on_vector=(j % 2 == 1))

@@ -43,8 +43,8 @@ def tile_trendattentionlayer_pa_kernel(
         stage = ctx.enter_context(tc.tile_pool(name="stage", bufs=2))
         mx = ctx.enter_context(tc.tile_pool(name="mx", bufs=2))
         logit_pool = ctx.enter_context(tc.tile_pool(name="logit_pool", bufs=5))
-        expo_pool = ctx.enter_context(tc.tile_pool(name="expo_pool", bufs=4))
-        low_pool = ctx.enter_context(tc.tile_pool(name="low_pool", bufs=4))
+        expo_pool = ctx.enter_context(tc.tile_pool(name="expo_pool", bufs=6))
+        low_pool = ctx.enter_context(tc.tile_pool(name="low_pool", bufs=6))
         gated_pool = ctx.enter_context(tc.tile_pool(name="gated_pool", bufs=14))
         small = ctx.enter_context(tc.tile_pool(name="small", bufs=4))
         psum_two = ctx.enter_context(tc.psum_pool(name="psum_two", bufs=2))
@@ -331,7 +331,7 @@ def tile_trendattentionlayer_pa_kernel(
             8: [("q", 1, 1, 2), ("val", 1, 0, 2), ("val", 1, 1, 2)],
             9: [], 10: [], 11: [],
         }
-        wv_plan = {1: [(0, 0, "S"), (1, 0, "S")], 2: [(0, 1, "S")], 3: [(1, 1, "S")]}
+        wv_plan = {0: [(0, 0, "V")], 1: [(1, 0, "V")], 2: [(0, 1, "V")], 3: [(1, 1, "V")]}
         v_plan = {
             4: [(0, 0, 0)], 5: [(0, 0, 1), (0, 1, 0)], 6: [(0, 1, 1), (0, 0, 2)], 7: [(0, 1, 2), (1, 0, 0)],
             8: [(1, 1, 0)], 9: [(1, 0, 1), (1, 1, 1)], 10: [(1, 0, 2), (1, 1, 2)],
@@ -347,10 +347,16 @@ def tile_trendattentionlayer_pa_kernel(
         pending = [(gather_words(turn(first[4])), first[4])]
 
         waiting = []
-        before = None
-        closing = None
+        past = []
         partial = None
         wv_pending = []
+        last = len(slots) - 1
+
+        def sum_columns(slot):
+            key, pair, expos, row_sum, lows, pieces = slot
+            column_sums(partials[key], pair, expos, lows, pieces)
+
+        partials = {}
         for n, (b, h, pair) in enumerate(slots):
             done = []
             exits = [(vb, vh, c) for vb, vh, vp in v_plan.get(n, []) for c in (2 * vp, 2 * vp + 1)]
@@ -360,29 +366,38 @@ def tile_trendattentionlayer_pa_kernel(
                 for half, place in enumerate(("k_raw0", "q_raw0")):
                     load("val", 1, half, slice(0, TILES), place)
             accs = [value_matmul(*x) for x in exits]
+            closing = None
+            if len(past) == 2:
+                slot = past.pop(0)
+                if slot[1] == 0:
+                    partials[slot[0]] = psum_one.tile(
+                        [P, TILES, PAIRS, 2, REPEAT], F32, name="partial", tag="partial"
+                    )
+                sum_columns(slot)
+                if slot[1] == PAIRS - 1:
+                    closing = slot[0]
             logits, row_max = logits_out(wides, narrow)
-            if before is not None:
-                pieces = row_weights(before[4], before[2])
+            if past:
+                past[0][5] = row_weights(past[0][3], past[0][1])
             store_logits(b, h, pair, logits)
             neg_max = negate(row_max)
+            if n == last:
+                past[0][4] += low_parts(past[0][2][1:], nc.vector)
             for group, bank in pending:
                 quantise(group, bank)
             pending = done
             for wv_grouped, g, hh in wv_pending:
                 quantise_wv(wv_grouped, g, hh)
-            if n + 1 < len(slots):
+            wv_pending = []
+            if n < last:
                 wides, narrow = logit_matmuls(*slots[n + 1])
             expos, row_sum = exponentials(logits, neg_max)
             if closing is not None:
-                close_head(closing, partial)
-                closing = None
-            lows = low_parts(expos, nc.gpsimd) if n + 1 < len(slots) else None
-            if before is not None:
-                if before[2] == 0:
-                    partial = psum_one.tile([P, TILES, PAIRS, 2, REPEAT], F32, name="partial", tag="partial")
-                column_sums(partial, before[2], before[3], before[5], pieces)
-                if before[2] == PAIRS - 1:
-                    closing = before[:2]
+                close_head(closing, partials[closing])
+            if n + 1 < last:
+                lows = low_parts(expos, nc.gpsimd)
+            else:
+                lows = low_parts(expos[:1], nc.gpsimd) if n < last else []
             for j, x in enumerate(exits):
                 waiting.append((add_bias(accs[j], x[1]),) + x)
             if n == 0:
@@ -390,23 +405,24 @@ def tile_trendattentionlayer_pa_kernel(
                     cols = slice(E * hh, E * (hh + 1))
                     spread = psum_flex.tile([P, BANK], F32, name="acc", tag="flex")
                     nc.tensor.matmul(out=spread[:], lhsT=ones[:], rhs=bias_rows[:, cols], start=True, stop=True)
-                    nc.vector.tensor_copy(out=bias_all[:, cols], in_=spread[:])
+                    nc.scalar.copy(out=bias_all[:, cols], in_=spread[:])
             wv_pending = [(regroup_wv(g, hh, e), g, hh) for g, hh, e in wv_plan.get(n, [])]
             ready = [w for w in waiting if w[1:3] in gates]
             for w in ready[:4]:
                 gate_and_store(*w)
                 waiting.remove(w)
-            before = (b, h, pair, expos, row_sum, lows)
+            past.append([(b, h), pair, expos, row_sum, lows, None])
 
-        expos = before[3]
-        lows = low_parts(expos[:1], nc.vector)
-        pieces = row_weights(before[4], before[2])
-        lows = lows + low_parts(expos[1:], nc.vector)
+        final = past[1]
+        final[4] = low_parts(final[2][:1], nc.vector)
+        final[5] = row_weights(final[3], final[1])
+        final[4] += low_parts(final[2][1:], nc.vector)
         ready = [w for w in waiting if w[1:3] in gates]
         for w in ready:
             gate_and_store(*w)
             waiting.remove(w)
-        column_sums(partial, before[2], expos, lows, pieces)
-        close_head(before[:2], partial)
+        sum_columns(past[0])
+        sum_columns(final)
+        close_head(final[0], partials[final[0]])
         for j, w in enumerate(waiting):
             gate_and_store(*w, on_vector=(j % 2 == 1))

@@ -23,7 +23,7 @@ TILES = L // P
 PAIRS = TILES // 2
 BANK = 512
 REST = S - BANK
-REPEAT = 8
+REPEAT = 14
 
 assert E == K_PASS and E == BANK and L == S
 assert all(TILES % stride == 0 for stride in STRIDES)
@@ -103,6 +103,8 @@ def tile_trendattentionlayer_pa_kernel(
         make_identity(nc, identity[:])
         ones = consts.tile([P, P], BF16)
         nc.vector.memset(ones[:], 1.0)
+        ones_wide = consts.tile([P, BANK], BF16)
+        nc.vector.memset(ones_wide[:], 1.0)
         stride_hits = consts.tile([P, TILES], F32)
         for r in range(TILES):
             hits = sum(1 for stride in STRIDES if r % stride == 0)
@@ -246,12 +248,16 @@ def tile_trendattentionlayer_pa_kernel(
         def high_halves(expo):
             return expo[:].bitcast(BF16).rearrange("p (s half) -> p s half", half=2)[:, :, 1]
 
-        def low_parts(expos, engine):
+        def low_part(engine, low, expo, cols):
+            engine.tensor_tensor(
+                out=low[:, cols], in0=expo[:, cols], in1=high_halves(expo)[:, cols], op=ALU.subtract
+            )
+
+        def new_lows():
             lows = []
-            for expo in expos:
+            for i in range(2):
                 low = low_pool.tile([P, S], BF16, name="low", tag="low")
                 lows.append(low)
-                engine.tensor_tensor(out=low[:], in0=expo[:], in1=high_halves(expo), op=ALU.subtract)
             return lows
 
         def row_weights(row_sum, pair):
@@ -336,6 +342,9 @@ def tile_trendattentionlayer_pa_kernel(
             4: [(0, 0, 0)], 5: [(0, 0, 1), (0, 1, 0)], 6: [(0, 1, 1), (0, 0, 2)], 7: [(0, 1, 2), (1, 0, 0)],
             8: [(1, 1, 0)], 9: [(1, 0, 1), (1, 1, 1)], 10: [(1, 0, 2), (1, 1, 2)],
         }
+        for j in range(5):
+            warm_up = psum_flex.tile([P, BANK], F32, name="acc", tag="flex")
+            nc.tensor.matmul(out=warm_up[:], lhsT=ones[:], rhs=bias_rows[:, 0:BANK] if 0 else ones_wide[:], start=True, stop=True)
         first = [("k", 0, 0, pair) for pair in range(PAIRS)] + [("q", 0, 0, 0), ("q", 0, 0, 1)]
         grouped = []
         for j, bank in enumerate(first[:4]):
@@ -381,10 +390,10 @@ def tile_trendattentionlayer_pa_kernel(
                 past[0][5] = row_weights(past[0][3], past[0][1])
             store_logits(b, h, pair, logits)
             neg_max = negate(row_max)
-            if n == last:
-                past[0][4] += low_parts(past[0][2][1:], nc.vector)
             for group, bank in pending:
                 quantise(group, bank)
+            if past:
+                low_part(nc.vector, past[0][4][1], past[0][2][1], slice(256, S))
             pending = done
             for wv_grouped, g, hh in wv_pending:
                 quantise_wv(wv_grouped, g, hh)
@@ -394,10 +403,10 @@ def tile_trendattentionlayer_pa_kernel(
             expos, row_sum = exponentials(logits, neg_max)
             if closing is not None:
                 close_head(closing, partials[closing])
-            if n + 1 < last:
-                lows = low_parts(expos, nc.gpsimd)
-            else:
-                lows = low_parts(expos[:1], nc.gpsimd) if n < last else []
+            lows = new_lows()
+            if n < last:
+                low_part(nc.gpsimd, lows[0], expos[0], slice(0, S))
+                low_part(nc.gpsimd, lows[1], expos[1], slice(0, 256))
             for j, x in enumerate(exits):
                 waiting.append((add_bias(accs[j], x[1]),) + x)
             if n == 0:
@@ -414,9 +423,9 @@ def tile_trendattentionlayer_pa_kernel(
             past.append([(b, h), pair, expos, row_sum, lows, None])
 
         final = past[1]
-        final[4] = low_parts(final[2][:1], nc.vector)
+        low_part(nc.vector, final[4][0], final[2][0], slice(0, S))
         final[5] = row_weights(final[3], final[1])
-        final[4] += low_parts(final[2][1:], nc.vector)
+        low_part(nc.vector, final[4][1], final[2][1], slice(0, S))
         ready = [w for w in waiting if w[1:3] in gates]
         for w in ready:
             gate_and_store(*w)
@@ -425,4 +434,4 @@ def tile_trendattentionlayer_pa_kernel(
         sum_columns(final)
         close_head(final[0], partials[final[0]])
         for j, w in enumerate(waiting):
-            gate_and_store(*w, on_vector=(j % 2 == 1))
+            gate_and_store(*w, on_vector=(j % 3 != 0))

@@ -52,6 +52,12 @@ def tile_trendattentionlayer_pa_kernel(
         psum_one = ctx.enter_context(tc.psum_pool(name="psum_one", bufs=1))
         ctx.enter_context(tc.manual_schedule())
 
+        ones = consts.tile([P, 256], BF16)
+        nc.vector.memset(ones[:], 1.0)
+        for j in range(7):
+            warm_up = psum_flex.tile([P, BANK], F32, name="warm_up", tag="flex")
+            nc.tensor.matmul(out=warm_up[:, 0:256], lhsT=ones[:, 0:P], rhs=ones[:], start=True, stop=True)
+
         def view(name, b):
             source, pattern = {
                 "k": (k_proj, "(c p) d -> p c d"),
@@ -101,10 +107,6 @@ def tile_trendattentionlayer_pa_kernel(
         nc.scalar.activation(out=warm[:], in_=warm[:], func=ACT.Exp)
         identity = consts.tile([P, P], F32)
         make_identity(nc, identity[:])
-        ones = consts.tile([P, P], BF16)
-        nc.vector.memset(ones[:], 1.0)
-        ones_wide = consts.tile([P, BANK], BF16)
-        nc.vector.memset(ones_wide[:], 1.0)
         stride_hits = consts.tile([P, TILES], F32)
         for r in range(TILES):
             hits = sum(1 for stride in STRIDES if r % stride == 0)
@@ -339,16 +341,18 @@ def tile_trendattentionlayer_pa_kernel(
         }
         wv_plan = {0: [(0, 0, "V")], 1: [(1, 0, "V")], 2: [(0, 1, "V")], 3: [(1, 1, "V")]}
         v_plan = {
-            4: [(0, 0, 0)], 5: [(0, 0, 1), (0, 1, 0)], 6: [(0, 1, 1), (0, 0, 2)], 7: [(0, 1, 2), (1, 0, 0)],
-            8: [(1, 1, 0)], 9: [(1, 0, 1), (1, 1, 1)], 10: [(1, 0, 2), (1, 1, 2)],
+            4: [(0, 0, 0), (0, 0, 1)],
+            5: [(0, 0, 2), (0, 0, 3), (0, 1, 0)],
+            6: [(0, 1, 1), (0, 1, 2), (0, 1, 3)],
+            7: [(0, 0, 4), (0, 0, 5), (0, 1, 4)],
+            8: [(0, 1, 5), (1, 0, 0), (1, 0, 1)],
+            9: [(1, 0, 2), (1, 0, 3), (1, 1, 0), (1, 1, 1), (1, 1, 2)],
+            10: [(1, 0, 4), (1, 0, 5), (1, 1, 3), (1, 1, 4), (1, 1, 5)],
         }
-        for j in range(5):
-            warm_up = psum_flex.tile([P, BANK], F32, name="acc", tag="flex")
-            nc.tensor.matmul(out=warm_up[:], lhsT=ones[:], rhs=bias_rows[:, 0:BANK] if 0 else ones_wide[:], start=True, stop=True)
         first = [("k", 0, 0, pair) for pair in range(PAIRS)] + [("q", 0, 0, 0), ("q", 0, 0, 1)]
         grouped = []
         for j, bank in enumerate(first[:4]):
-            grouped.append(gather_words(turn(bank), on_vector=(j % 2 == 1)))
+            grouped.append(gather_words(turn(bank), on_vector=(j == 1)))
             if j >= 1:
                 quantise(grouped[j - 1], first[j - 1])
         quantise(grouped[-1], first[3])
@@ -368,13 +372,28 @@ def tile_trendattentionlayer_pa_kernel(
         partials = {}
         for n, (b, h, pair) in enumerate(slots):
             done = []
-            exits = [(vb, vh, c) for vb, vh, vp in v_plan.get(n, []) for c in (2 * vp, 2 * vp + 1)]
-            for bank in prep[n]:
+            exits = list(v_plan.get(n, []))
+            started = []
+
+            def start_product():
+                if exits:
+                    x = exits.pop(0)
+                    started.append((value_matmul(*x),) + x)
+
+            def finish_product():
+                if started:
+                    acc, vb, vh, c = started.pop(0)
+                    waiting.append((add_bias(acc, vh), vb, vh, c))
+
+            for j, bank in enumerate(prep[n]):
+                if j == 2:
+                    start_product()
                 done.append((gather_words(turn(bank)), bank))
             if n == 0:
                 for half, place in enumerate(("k_raw0", "q_raw0")):
                     load("val", 1, half, slice(0, TILES), place)
-            accs = [value_matmul(*x) for x in exits]
+            while exits and len(started) < (2 if prep[n] else 4):
+                start_product()
             closing = None
             if len(past) == 2:
                 slot = past.pop(0)
@@ -390,10 +409,13 @@ def tile_trendattentionlayer_pa_kernel(
                 past[0][5] = row_weights(past[0][3], past[0][1])
             store_logits(b, h, pair, logits)
             neg_max = negate(row_max)
+            if prep[n]:
+                finish_product()
+                start_product()
             for group, bank in pending:
                 quantise(group, bank)
             if past:
-                low_part(nc.vector, past[0][4][1], past[0][2][1], slice(256, S))
+                low_part(nc.vector, past[0][4][1], past[0][2][1], slice(384, S))
             pending = done
             for wv_grouped, g, hh in wv_pending:
                 quantise_wv(wv_grouped, g, hh)
@@ -406,14 +428,15 @@ def tile_trendattentionlayer_pa_kernel(
             lows = new_lows()
             if n < last:
                 low_part(nc.gpsimd, lows[0], expos[0], slice(0, S))
-                low_part(nc.gpsimd, lows[1], expos[1], slice(0, 256))
-            for j, x in enumerate(exits):
-                waiting.append((add_bias(accs[j], x[1]),) + x)
+                low_part(nc.gpsimd, lows[1], expos[1], slice(0, 384))
+            while started:
+                finish_product()
+                start_product()
             if n == 0:
                 for hh in range(H):
                     cols = slice(E * hh, E * (hh + 1))
                     spread = psum_flex.tile([P, BANK], F32, name="acc", tag="flex")
-                    nc.tensor.matmul(out=spread[:], lhsT=ones[:], rhs=bias_rows[:, cols], start=True, stop=True)
+                    nc.tensor.matmul(out=spread[:], lhsT=ones[:, 0:P], rhs=bias_rows[:, cols], start=True, stop=True)
                     nc.scalar.copy(out=bias_all[:, cols], in_=spread[:])
             wv_pending = [(regroup_wv(g, hh, e), g, hh) for g, hh, e in wv_plan.get(n, [])]
             ready = [w for w in waiting if w[1:3] in gates]

from contextlib import ExitStack

import concourse.mybir as mybir
from concourse.masks import make_identity

F32 = mybir.dt.float32
BF16 = mybir.dt.bfloat16
U32 = mybir.dt.uint32
U8 = mybir.dt.uint8
FP8X4 = mybir.dt.float8_e4m3fn_x4
ALU = mybir.AluOpType
ACT = mybir.ActivationFunctionType

B, L, S, D, H = 2, 768, 768, 1024, 2
E = D // H
STRIDES = (1, 2, 3)

P = 128
PACK = 4
K_PASS = P * PACK
PASSES = D // K_PASS
TILES = L // P
PAIRS = TILES // 2
BANK = 512
REST = S - BANK
REPEAT = 14

assert E == K_PASS and E == BANK and L == S
assert all(TILES % stride == 0 for stride in STRIDES)

FLOPS = 2 * B * H * L * S * E + 2 * B * S * D * D


def tile_trendattentionlayer_pa_kernel(
    tc, q_proj, k_proj, values, Wv, bv, out_0, out_1, out_2, out_3
):
    nc = tc.nc
    attn_out = {1: out_1, 2: out_2, 3: out_3}

    with ExitStack() as ctx:
        consts = ctx.enter_context(tc.tile_pool(name="consts", bufs=1))
        raw = ctx.enter_context(tc.tile_pool(name="raw", bufs=1))
        stage = ctx.enter_context(tc.tile_pool(name="stage", bufs=2))
        mx = ctx.enter_context(tc.tile_pool(name="mx", bufs=2))
        logit_pool = ctx.enter_context(tc.tile_pool(name="logit_pool", bufs=5))
        expo_pool = ctx.enter_context(tc.tile_pool(name="expo_pool", bufs=6))
        low_pool = ctx.enter_context(tc.tile_pool(name="low_pool", bufs=6))
        gated_pool = ctx.enter_context(tc.tile_pool(name="gated_pool", bufs=14))
        small = ctx.enter_context(tc.tile_pool(name="small", bufs=4))
        psum_two = ctx.enter_context(tc.psum_pool(name="psum_two", bufs=2))
        psum_flex = ctx.enter_context(tc.psum_pool(name="psum_flex", bufs=4))
        psum_one = ctx.enter_context(tc.psum_pool(name="psum_one", bufs=1))
        ctx.enter_context(tc.manual_schedule())

        ones = consts.tile([P, 256], BF16)
        nc.vector.memset(ones[:], 1.0)
        for j in range(7):
            warm_up = psum_flex.tile([P, BANK], F32, name="warm_up", tag="flex")
            nc.tensor.matmul(out=warm_up[:, 0:256], lhsT=ones[:, 0:P], rhs=ones[:], start=True, stop=True)

        def view(name, b):
            source, pattern = {
                "k": (k_proj, "(c p) d -> p c d"),
                "q": (q_proj, "(p r) d -> p r d"),
                "val": (values, "(c p) d -> p c d"),
            }[name]
            return source[b].rearrange(pattern, p=P)

        raws = {}

        def load(name, b, h, tiles, place=None):
            if (name, b, h) not in raws:
                rows = raw.tile([P, TILES, E], BF16, name=name + "_raw", tag=place or "%s_raw%d" % (name, h))
                raws[(name, b, h)] = (rows, 0)
            rows = raws[(name, b, h)][0]
            nc.sync.dma_start(out=rows[:, tiles, :], in_=view(name, b)[:, tiles, E * h : E * (h + 1)])

        def load_whole(name, b):
            rows = raw.tile([P, TILES, D], BF16, name=name + "_raw", tag="%s_raw_all%d" % (name, b))
            nc.sync.dma_start(out=rows[:], in_=view(name, b))
            for half in range(D // E):
                raws[(name, b, half)] = (rows, E * half)

        for pair in range(PAIRS):
            load("k", 0, 0, slice(2 * pair, 2 * pair + 2))
        load("q", 0, 0, slice(0, 2))
        load("q", 0, 0, slice(2, TILES))
        bias_rows = consts.tile([P, D], BF16)
        nc.vector.memset(bias_rows[:], 0.0)
        nc.sync.dma_start(out=bias_rows[0:1, :], in_=bv.rearrange("(o d) -> o d", o=1))
        load("k", 0, 1, slice(0, TILES))
        load("q", 0, 1, slice(0, TILES))
        wv_raws = []
        for g in range(PASSES):
            wv_raw = consts.tile([P, PACK, D], BF16, name="wv_raw", tag="wv_raw%d" % g)
            wv_raws.append(wv_raw)
            nc.sync.dma_start(
                out=wv_raw[:].rearrange("p t n -> p (t n)"),
                in_=Wv[K_PASS * g : K_PASS * (g + 1), :].rearrange("(p t) n -> p (t n)", t=PACK),
            )
        load_whole("val", 0)
        for name in ("k", "q"):
            load_whole(name, 1)

        warm = consts.tile([P, 1], F32)
        nc.vector.memset(warm[:], 0.0)
        nc.scalar.activation(out=warm[:], in_=warm[:], func=ACT.Exp)
        identity = consts.tile([P, P], F32)
        make_identity(nc, identity[:])
        stride_hits = consts.tile([P, TILES], F32)
        for r in range(TILES):
            hits = sum(1 for stride in STRIDES if r % stride == 0)
            nc.vector.memset(stride_hits[:, r : r + 1], float(hits))
        hits_per_stride = consts.tile([P, TILES], F32)
        nc.vector.tensor_scalar_mul(out=hits_per_stride[:], in0=stride_hits[:], scalar1=1.0 / len(STRIDES))
        bias_all = consts.tile([P, D], F32)
        wv_codes = consts.tile([P, PASSES, D], U32, align_bytes=64)
        wv_scales = consts.tile([P, PASSES, D], U8, align_bytes=64)

        operands = {}

        def operand(name, b, half):
            key = (name, b, half)
            if key not in operands:
                tag = name if name != "val" else "val%d" % half
                codes = mx.tile([P, S], U32, name="codes", tag=tag + "_codes", align_bytes=64)
                scales = mx.tile([P, S], U8, name="scales", tag=tag + "_scales", align_bytes=64)
                operands[key] = (codes, scales)
            return operands[key]

        def turn(bank):
            name, b, half, pair = bank
            rows, feature = raws[(name, b, half)]
            words = rows[:].bitcast(F32)
            turned = psum_flex.tile([P, 2, 2, P], F32, name="turned", tag="flex")
            for i in range(2):
                for u in range(2):
                    first = feature // 2
                    nc.tensor.transpose(
                        turned[:, i, u, :],
                        words[:, 2 * pair + i, first + u : first + K_PASS // 2 : 2],
                        identity[:],
                    )
            return turned

        def gather_words(turned, on_vector=False):
            grouped = stage.tile([P, 2 * P, PACK], BF16, name="grouped", tag="grouped", bufs=8, align_bytes=64)
            out = grouped[:].bitcast(F32).rearrange("p (i r) u -> p i r u", i=2)
            source = turned[:].rearrange("p i u r -> p i r u")
            if on_vector:
                nc.vector.tensor_copy(out=out, in_=source)
            else:
                nc.scalar.copy(out=out, in_=source)
            return grouped

        def quantise(grouped, bank):
            name, b, half, pair = bank
            codes, scales = operand(name, b, half)
            cols = slice(2 * P * pair, 2 * P * (pair + 1))
            nc.vector.quantize_mx(
                out=codes[:, cols].bitcast(FP8X4), scales=scales[:, cols],
                in_=grouped[:].rearrange("p s t -> p (s t)"),
            )

        def regroup_wv(g, h, engine):
            wv_grouped = stage.tile([P, E, PACK], BF16, name="wv_grouped", tag="wv_grouped", align_bytes=64)
            out = wv_grouped[:].rearrange("p (c i) t -> p c t i", i=4)
            source = wv_raws[g][:, :, E * h : E * (h + 1)].rearrange("p t (c i) -> p c t i", i=4)
            if engine == "S":
                nc.scalar.copy(out=out, in_=source)
            else:
                nc.vector.tensor_copy(out=out, in_=source)
            return wv_grouped

        def quantise_wv(wv_grouped, g, h):
            cols = slice(E * h, E * (h + 1))
            nc.vector.quantize_mx(
                out=wv_codes[:, g, cols].bitcast(FP8X4), scales=wv_scales[:, g, cols],
                in_=wv_grouped[:].rearrange("p n t -> p (n t)"),
            )

        def logit_matmuls(b, h, pair):
            q_codes, q_scales = operand("q", b, h)
            k_codes, k_scales = operand("k", b, h)
            narrow = psum_one.tile([P, 2, REST], F32, name="narrow", tag="narrow")
            wides = []
            for i in range(2):
                rows = slice(P * (2 * pair + i), P * (2 * pair + i + 1))
                wide = psum_two.tile([P, BANK], F32, name="wide", tag="wide")
                wides.append(wide)
                for target, cols in ((wide[:], slice(0, BANK)), (narrow[:, i, :], slice(BANK, S))):
                    nc.tensor.matmul_mx(
                        out=target,
                        lhsT=q_codes[:, rows].bitcast(FP8X4), lhsT_scale=q_scales[:, rows],
                        rhs=k_codes[:, cols].bitcast(FP8X4), rhs_scale=k_scales[:, cols],
                        start=True, stop=True,
                    )
            return wides, narrow

        def logits_out(wides, narrow):
            logits = logit_pool.tile([P, 2, S], F32, name="logits", tag="logits")
            wide_max = small.tile([P, 2], F32, name="wide_max", tag="wide_max")
            row_max = small.tile([P, 2], F32, name="row_max", tag="row_max")
            for i in range(2):
                nc.vector.tensor_scalar(
                    out=logits[:, i, 0:BANK], in0=wides[i][:], scalar1=1.0, scalar2=None,
                    op0=ALU.mult, op1=ALU.max, accum_out=wide_max[:, i : i + 1],
                )
            for i in range(2):
                nc.vector.tensor_scalar(
                    out=logits[:, i, BANK:S], in0=narrow[:, i, :], scalar1=1.0,
                    scalar2=wide_max[:, i : i + 1],
                    op0=ALU.mult, op1=ALU.max, accum_out=row_max[:, i : i + 1],
                )
            return logits, row_max

        def store_logits(b, h, pair, logits):
            nc.sync.dma_start(
                out=out_1[b, h].rearrange("(a r) s -> a r s", r=TILES)[:, 2 * pair : 2 * pair + 2, :],
                in_=logits[:],
            )
            for stride in STRIDES[1:]:
                for i in range(2):
                    r = 2 * pair + i
                    if r % stride == 0:
                        nc.sync.dma_start(
                            out=attn_out[stride][b, h].rearrange("(a m) s -> a m s", m=TILES // stride)[
                                :, r // stride, :
                            ],
                            in_=logits[:, i, :],
                        )

        def negate(row_max):
            neg_max = small.tile([P, 2], F32, name="neg_max", tag="neg_max")
            nc.scalar.activation(out=neg_max[:], in_=row_max[:], func=ACT.Copy, scale=-1.0)
            return neg_max

        def exponentials(logits, neg_max):
            row_sum = small.tile([P, 2], F32, name="row_sum", tag="row_sum")
            expos = []
            for i in range(2):
                expo = expo_pool.tile([P, S], F32, name="expo", tag="expo")
                expos.append(expo)
                nc.scalar.activation(
                    out=expo[:], in_=logits[:, i, :], func=ACT.Exp,
                    bias=neg_max[:, i : i + 1], scale=1.0, accum_out=row_sum[:, i : i + 1],
                )
            return expos, row_sum

        def high_halves(expo):
            return expo[:].bitcast(BF16).rearrange("p (s half) -> p s half", half=2)[:, :, 1]

        def low_part(engine, low, expo, cols):
            engine.tensor_tensor(
                out=low[:, cols], in0=expo[:, cols], in1=high_halves(expo)[:, cols], op=ALU.subtract
            )

        def new_lows():
            lows = []
            for i in range(2):
                low = low_pool.tile([P, S], BF16, name="low", tag="low")
                lows.append(low)
            return lows

        def row_weights(row_sum, pair):
            inv_sum = small.tile([P, 2], F32, name="inv_sum", tag="inv_sum")
            nc.vector.reciprocal(out=inv_sum[:], in_=row_sum[:])
            weight = small.tile([P, 2], F32, name="weight", tag="weight")
            nc.gpsimd.tensor_tensor(
                out=weight[:], in0=inv_sum[:], in1=hits_per_stride[:, 2 * pair : 2 * pair + 2], op=ALU.mult
            )
            repeated = weight[:].unsqueeze(2).to_broadcast([P, 2, REPEAT])
            pieces = small.tile([P, 2, 2, REPEAT], BF16, name="pieces", tag="pieces")
            nc.gpsimd.tensor_scalar(
                out=pieces[:, :, 0, :], in0=repeated, scalar1=1.0, scalar2=0.0, op0=ALU.mult, op1=ALU.add
            )
            nc.gpsimd.tensor_tensor(out=pieces[:, :, 1, :], in0=repeated, in1=pieces[:, :, 0, :], op=ALU.subtract)
            return pieces

        def column_sums(partial, pair, expos, lows, pieces):
            for c in range(TILES):
                chunk = slice(P * c, P * (c + 1))
                for i in range(2):
                    for part, stationary in enumerate((high_halves(expos[i])[:, chunk], lows[i][:, chunk])):
                        nc.tensor.matmul(
                            out=partial[:, c, pair].rearrange("p w r -> p (w r)"),
                            lhsT=stationary,
                            rhs=pieces[:, i].rearrange("p w r -> p (w r)"),
                            start=(i == 0 and part == 0), stop=(i == 1 and part == 1),
                        )

        def close_head(key, partial):
            col_sum = small.tile([P, TILES], F32, name="col_sum", tag="col_sum")
            nc.vector.tensor_reduce(
                out=col_sum[:], in_=partial[:, :, :, :, 0], axis=mybir.AxisListType.XY, op=ALU.add
            )
            gates[key] = col_sum

        def value_matmul(b, h, c):
            rows = slice(P * c, P * (c + 1))
            cols = slice(E * h, E * (h + 1))
            acc = psum_flex.tile([P, BANK], F32, name="acc", tag="flex")
            for g in range(PASSES):
                val_codes, val_scales = operand("val", b, g)
                nc.tensor.matmul_mx(
                    out=acc[:],
                    lhsT=val_codes[:, rows].bitcast(FP8X4), lhsT_scale=val_scales[:, rows],
                    rhs=wv_codes[:, g, cols].bitcast(FP8X4), rhs_scale=wv_scales[:, g, cols],
                    start=(g == 0), stop=(g == PASSES - 1),
                )
            return acc

        def add_bias(acc, h):
            gated = gated_pool.tile([P, E], F32, name="gated", tag="gated")
            nc.vector.tensor_tensor(
                out=gated[:], in0=acc[:], in1=bias_all[:, E * h : E * (h + 1)], op=ALU.add
            )
            return gated

        def gate_and_store(gated, b, h, c, on_vector=False):
            gate = gates[(b, h)][:, c : c + 1]
            if on_vector:
                nc.vector.tensor_scalar_mul(out=gated[:], in0=gated[:], scalar1=gate)
            else:
                nc.scalar.activation(out=gated[:], in_=gated[:], func=ACT.Copy, scale=gate)
            nc.sync.dma_start(out=out_0[b, P * c : P * (c + 1), E * h : E * (h + 1)], in_=gated[:])

        slots = [(b, h, pair) for b in range(B) for h in range(H) for pair in range(PAIRS)]
        gates = {}
        prep = {
            0: [("q", 0, 0, 2), ("k", 0, 1, 0)],
            1: [("k", 0, 1, 1), ("k", 0, 1, 2), ("q", 0, 1, 0)],
            2: [("q", 0, 1, 1), ("q", 0, 1, 2), ("val", 0, 0, 0), ("val", 0, 1, 0)],
            3: [("k", 1, 0, 0), ("k", 1, 0, 1), ("val", 0, 0, 1), ("val", 0, 1, 1)],
            4: [("k", 1, 0, 2), ("q", 1, 0, 0), ("val", 0, 0, 2), ("val", 0, 1, 2)],
            5: [("q", 1, 0, 1), ("q", 1, 0, 2), ("val", 1, 0, 0), ("val", 1, 1, 0)],
            6: [("k", 1, 1, 0), ("k", 1, 1, 1), ("k", 1, 1, 2), ("q", 1, 1, 0)],
            7: [("q", 1, 1, 1), ("val", 1, 0, 1), ("val", 1, 1, 1)],
            8: [("q", 1, 1, 2), ("val", 1, 0, 2), ("val", 1, 1, 2)],
            9: [], 10: [], 11: [],
        }
        wv_plan = {0: [(0, 0, "V")], 1: [(1, 0, "V")], 2: [(0, 1, "V")], 3: [(1, 1, "V")]}
        v_plan = {
            4: [(0, 0, 0), (0, 0, 1)],
            5: [(0, 0, 2), (0, 0, 3), (0, 1, 0)],
            6: [(0, 1, 1), (0, 1, 2), (0, 1, 3)],
            7: [(0, 0, 4), (0, 0, 5), (0, 1, 4)],
            8: [(0, 1, 5), (1, 0, 0), (1, 0, 1)],
            9: [(1, 0, 2), (1, 0, 3), (1, 1, 0), (1, 1, 1), (1, 1, 2)],
            10: [(1, 0, 4), (1, 0, 5), (1, 1, 3), (1, 1, 4), (1, 1, 5)],
        }
        first = [("k", 0, 0, pair) for pair in range(PAIRS)] + [("q", 0, 0, 0), ("q", 0, 0, 1)]
        grouped = []
        for j, bank in enumerate(first[:4]):
            grouped.append(gather_words(turn(bank), on_vector=(j == 1)))
            if j >= 1:
                quantise(grouped[j - 1], first[j - 1])
        quantise(grouped[-1], first[3])
        wides, narrow = logit_matmuls(0, 0, 0)
        pending = [(gather_words(turn(first[4])), first[4])]

        waiting = []
        past = []
        partial = None
        wv_pending = []
        last = len(slots) - 1

        def sum_columns(slot):
            key, pair, expos, row_sum, lows, pieces = slot
            column_sums(partials[key], pair, expos, lows, pieces)

        partials = {}
        for n, (b, h, pair) in enumerate(slots):
            done = []
            exits = list(v_plan.get(n, []))
            started = []

            def start_product():
                if exits:
                    x = exits.pop(0)
                    started.append((value_matmul(*x),) + x)

            def finish_product():
                if started:
                    acc, vb, vh, c = started.pop(0)
                    waiting.append((add_bias(acc, vh), vb, vh, c))

            for j, bank in enumerate(prep[n]):
                if j == 2:
                    start_product()
                done.append((gather_words(turn(bank)), bank))
            if n == 0:
                for half, place in enumerate(("k_raw0", "q_raw0")):
                    load("val", 1, half, slice(0, TILES), place)
            while exits and len(started) < (2 if prep[n] else 4):
                start_product()
            closing = None
            if len(past) == 2:
                slot = past.pop(0)
                if slot[1] == 0:
                    partials[slot[0]] = psum_one.tile(
                        [P, TILES, PAIRS, 2, REPEAT], F32, name="partial", tag="partial"
                    )
                sum_columns(slot)
                if slot[1] == PAIRS - 1:
                    closing = slot[0]
            logits, row_max = logits_out(wides, narrow)
            if past:
                past[0][5] = row_weights(past[0][3], past[0][1])
            store_logits(b, h, pair, logits)
            neg_max = negate(row_max)
            if prep[n]:
                finish_product()
                start_product()
            for group, bank in pending:
                quantise(group, bank)
            if past:
                low_part(nc.vector, past[0][4][1], past[0][2][1], slice(384, S))
            pending = done
            for wv_grouped, g, hh in wv_pending:
                quantise_wv(wv_grouped, g, hh)
            wv_pending = []
            if n < last:
                wides, narrow = logit_matmuls(*slots[n + 1])
            expos, row_sum = exponentials(logits, neg_max)
            if closing is not None:
                close_head(closing, partials[closing])
            lows = new_lows()
            if n < last:
                low_part(nc.gpsimd, lows[0], expos[0], slice(0, S))
                low_part(nc.gpsimd, lows[1], expos[1], slice(0, 384))
            while started:
                finish_product()
                start_product()
            if n == 0:
                for hh in range(H):
                    cols = slice(E * hh, E * (hh + 1))
                    spread = psum_flex.tile([P, BANK], F32, name="acc", tag="flex")
                    nc.tensor.matmul(out=spread[:], lhsT=ones[:, 0:P], rhs=bias_rows[:, cols], start=True, stop=True)
                    nc.scalar.copy(out=bias_all[:, cols], in_=spread[:])
            wv_pending = [(regroup_wv(g, hh, e), g, hh) for g, hh, e in wv_plan.get(n, [])]
            ready = [w for w in waiting if w[1:3] in gates]
            for w in ready[:4]:
                gate_and_store(*w)
                waiting.remove(w)
            past.append([(b, h), pair, expos, row_sum, lows, None])

        final = past[1]
        low_part(nc.vector, final[4][0], final[2][0], slice(0, S))
        final[5] = row_weights(final[3], final[1])
        low_part(nc.vector, final[4][1], final[2][1], slice(0, S))
        ready = [w for w in waiting if w[1:3] in gates]
        for w in ready:
            gate_and_store(*w)
            waiting.remove(w)
        sum_columns(past[0])
        sum_columns(final)
        close_head(final[0], partials[final[0]])
        for j, w in enumerate(waiting):
            gate_and_store(*w, on_vector=(j % 3 != 0))
